import numpy as np
import ml_dtypes


def mxq(x, axis, fmt="e4m3"):
    dtype, down = {"e4m3": (ml_dtypes.float8_e4m3fn, 7), "e5m2": (ml_dtypes.float8_e5m2, 14)}[fmt]
    v = np.moveaxis(np.asarray(x, np.float32).astype(ml_dtypes.bfloat16).astype(np.float64), axis, -1)
    blocks = v.reshape(v.shape[:-1] + (-1, 32))
    amax = np.abs(blocks).max(-1, keepdims=True)
    byte = np.maximum(np.where(amax > 0, np.frexp(amax)[1] - 1 + 127, 0) - down, 1)
    scale = np.exp2(byte - 127.0)
    codes = (blocks / scale).astype(np.float32).astype(dtype).astype(np.float64)
    return np.moveaxis((codes * scale).reshape(v.shape), -1, axis)


WIDE = False


def mx_kscale(k):
    if not WIDE:
        return np.ones(k)
    levels = np.array([10, -10, 5, -5, 0])
    a = np.random.permutation(np.resize(levels, k // 512 * 4)).reshape(k // 512, 4)
    idx = np.arange(k)
    return np.exp2(a[idx // 512, idx % 128 // 32])


BF16 = ml_dtypes.bfloat16


def bf(x):
    return np.asarray(x, np.float32).astype(BF16)


def f64(x):
    return np.asarray(x).astype(np.float64)


E2M1 = np.array([0.0, 0.5, 1.0, 1.5, 2.0, 3.0, 4.0, 6.0, -0.0, -0.5, -1.0, -1.5, -2.0, -3.0, -4.0, -6.0])


def pack_weight(w, fmt):
    k, n = w.shape
    w = f64(bf(w)).reshape(k // 32, 32, n)
    amax = np.abs(w).max(1)
    if fmt == "e4m3":
        byte = np.frexp(amax)[1] - 1 + 127 - 7
    else:
        mant, ex = np.frexp(amax / 6.0)
        byte = np.where(mant > 0.5, ex, ex - 1) + 127
    byte = np.clip(np.where(amax > 0, byte, 1), 1, 254)
    scaled = (w * np.exp2(127.0 - byte)[:, None, :]).reshape(k, n).astype(np.float32)
    by_word = np.ascontiguousarray(scaled.reshape(k // 512, 128, 4, n).transpose(0, 1, 3, 2))
    if fmt == "e4m3":
        words = by_word.astype(ml_dtypes.float8_e4m3fn).view(np.uint8)
    else:
        c = by_word.astype(ml_dtypes.float4_e2m1fn).view(np.uint8) & 0xF
        words = c[..., 0::2] | (c[..., 1::2] << 4)
    return np.ascontiguousarray(words), np.ascontiguousarray(byte.astype(np.uint8).reshape(k // 512, 16, n))


def unpack_weight(words, scales, fmt):
    g, p, n, _ = words.shape
    if fmt == "e4m3":
        vals = np.ascontiguousarray(words).view(ml_dtypes.float8_e4m3fn).astype(np.float64)
    else:
        nib = np.empty((g, p, n, 4), np.uint8)
        nib[..., 0::2] = words & 0xF
        nib[..., 1::2] = words >> 4
        vals = E2M1[nib]
    vals = vals * np.repeat(np.exp2(scales.astype(np.float64) - 127.0), 8, axis=1)[..., None]
    return vals.transpose(0, 1, 3, 2).reshape(g * 512, n)

def pack4(w):
    words, scales = pack_weight(w, "e2m1")
    return words.reshape(words.shape[0], 128, -1), scales


def unpack4(words, scales):
    return unpack_weight(words.reshape(words.shape[0], 128, -1, 2), scales, "e2m1")


B, H, W, FI, FO = 4, 32, 32, 512, 1024

OFFSETS = [(-1, 0), (1, 0), (0, -1), (0, 1), (-1, -1), (-1, 1), (1, -1), (1, 1)]


def setup_inputs():
    s = mx_kscale(FI)
    X = bf(np.random.standard_normal((B, H * W, FI)) * 0.5 * s)
    Wm_words, Wm_scales = pack4(np.random.standard_normal((FI, FO)) / np.sqrt(FI) / s[:, None])
    b = bf(np.random.standard_normal(FO) * 0.2)
    return {"X": X,
            "Wm_words": Wm_words,
            "Wm_scales": Wm_scales,
            "b": b,
            "H": H, "W": W}


def reference(X, Wm_words, Wm_scales, b, H, W):
    X = f64(X)
    Bn, N, F = X.shape
    Xg = X.reshape(Bn, H, W, F)
    P = np.pad(Xg, ((0, 0), (1, 1), (1, 1), (0, 0)))
    AX = P[:, 1 + OFFSETS[0][0]:1 + OFFSETS[0][0] + H,
           1 + OFFSETS[0][1]:1 + OFFSETS[0][1] + W, :]
    for dr, dc in OFFSETS[1:]:
        AX = AX + P[:, 1 + dr:1 + dr + H, 1 + dc:1 + dc + W, :]
    AX = AX.reshape(Bn, N, F)
    return (mxq(AX, 2, "e4m3") @ unpack4(Wm_words, Wm_scales)) + f64(b)

@@ -1,0 +1,195 @@
+from contextlib import ExitStack
+
+import concourse.mybir as mybir
+from concourse.masks import make_identity
+
+F32 = mybir.dt.float32
+BF16 = mybir.dt.bfloat16
+I32 = mybir.dt.int32
+U32 = mybir.dt.uint32
+U8 = mybir.dt.uint8
+FP8X4 = mybir.dt.float8_e4m3fn_x4
+FP4X4 = mybir.dt.float4_e2m1fn_x4
+ADD = mybir.AluOpType.add
+
+P = 128
+PACK = 4
+N_BANK = 512
+
+FLOPS = 2 * 4 * 1024 * 512 * 1024
+
+
+def tile_graphconvlayer_kernel(tc, X, Wm_words, Wm_scales, b, H, W, out):
+    nc = tc.nc
+    images, nodes, features = X.shape
+    outputs = out.shape[2]
+    assert features == P * PACK and nodes == H * W and P % W == 0
+    tile_rows = P // W
+    half_nodes = P // 2
+    windows = H // 2
+    chunk_rows = 2 * tile_rows
+    chunk_tiles = 2
+    chunk_windows = 2 * chunk_tiles
+    chunks = H // chunk_rows
+    tensor_images = images - 1
+    last = images - 1
+
+    with ExitStack() as ctx:
+        const = ctx.enter_context(tc.tile_pool(name="const", bufs=1))
+        xin = ctx.enter_context(tc.tile_pool(name="xin", bufs=1))
+        elem = ctx.enter_context(tc.tile_pool(name="elem", bufs=1))
+        ring_pool = ctx.enter_context(tc.tile_pool(name="ring", bufs=2))
+        late = ctx.enter_context(tc.tile_pool(name="late", bufs=chunks))
+        stage = ctx.enter_context(tc.tile_pool(name="stage", bufs=3))
+        result = ctx.enter_context(tc.tile_pool(name="result", bufs=10))
+        psum_sums = ctx.enter_context(tc.psum_pool(name="psum_sums", bufs=2))
+        psum_words = ctx.enter_context(tc.psum_pool(name="psum_words", bufs=2))
+        psum_acc = ctx.enter_context(tc.psum_pool(name="psum_acc", bufs=4))
+
+        w_scales = const.tile([P, outputs], U8, align_bytes=64)
+        nc.vector.memset(w_scales[:].bitcast(I32), 0)
+        w_words = const.tile([P, 2 * outputs], U8, align_bytes=64)
+
+        def first_row(d):
+            return min(max(2 * d - 1, 0), H - tile_rows)
+
+        x_windows = [xin.tile([P, windows, features], BF16, name="x_image%d" % i) for i in range(tensor_images)]
+
+        def load_windows(i, g):
+            for d in range(chunk_windows * g, chunk_windows * (g + 1)):
+                node = W * first_row(d)
+                nc.sync.dma_start(out=x_windows[i][:, d, :], in_=X[i, node : node + P, :])
+
+        for quadrant in range(4):
+            nc.sync.dma_start(
+                out=w_scales[32 * quadrant : 32 * quadrant + 4, :].bitcast(I32),
+                in_=Wm_scales[0, 4 * quadrant : 4 * quadrant + 4, :].bitcast(I32),
+            )
+        load_windows(0, 0)
+        nc.sync.dma_start(out=w_words[:].bitcast(I32), in_=Wm_words[0].bitcast(I32))
+        bias = const.tile([P, outputs], BF16)
+        nc.scalar.dma_start(out=bias[:], in_=b.partition_broadcast(P))
+        x_last = xin.tile([P, nodes // P, features], BF16)
+        for g in range(chunks):
+            first = chunk_tiles * g
+            nc.sync.dma_start(
+                out=x_last[:, first : first + chunk_tiles, :],
+                in_=X[last, P * first : P * (first + chunk_tiles), :].rearrange("(j p) f -> p j f", p=P),
+            )
+        for i in range(tensor_images):
+            for g in range(chunks):
+                if (i, g) != (0, 0):
+                    load_windows(i, g)
+
+        ident = const.tile([P, P], F32)
+        make_identity(nc, ident[:])
+        ident_grid = ident[:].rearrange("p (r c) -> p r c", c=W)
+        same_row = const.tile([P, tile_rows, W], F32)
+        nc.vector.tensor_copy(out=same_row[:], in_=ident_grid)
+        nc.vector.tensor_add(out=same_row[:, :, 1:W], in0=same_row[:, :, 1:W], in1=ident_grid[:, :, 0 : W - 1])
+        nc.vector.tensor_add(out=same_row[:, :, 0 : W - 1], in0=same_row[:, :, 0 : W - 1], in1=ident_grid[:, :, 1:W])
+        around = const.tile([P, tile_rows, W], F32)
+        nc.vector.tensor_sub(out=around[:], in0=same_row[:], in1=ident_grid)
+        nc.vector.tensor_add(out=around[:, 1:tile_rows, :], in0=around[:, 1:tile_rows, :], in1=same_row[:, 0 : tile_rows - 1, :])
+        nc.vector.tensor_add(out=around[:, 0 : tile_rows - 1, :], in0=around[:, 0 : tile_rows - 1, :], in1=same_row[:, 1:tile_rows, :])
+        neighbours = const.tile([P, P], BF16)
+        nc.vector.tensor_copy(out=neighbours[:], in_=around[:].rearrange("p r c -> p (r c)"))
+
+        def multiply_and_store(grouped, i, g):
+            codes = stage.tile([P, chunk_tiles * P], U32, align_bytes=64)
+            scales = stage.tile([P, chunk_tiles * P], U8, align_bytes=64)
+            nc.vector.quantize_mx(
+                out=codes[:].bitcast(FP8X4),
+                scales=scales[:],
+                in_=grouped[:].rearrange("p j n t -> p (j n t)"),
+            )
+            for j in range(chunk_tiles):
+                rows = result.tile([P, outputs], F32)
+                node_cols = slice(P * j, P * (j + 1))
+                for h in range(outputs // N_BANK):
+                    acc = psum_acc.tile([P, N_BANK], F32)
+                    nc.tensor.matmul_mx(
+                        out=acc[:],
+                        lhsT=codes[:, node_cols].bitcast(FP8X4),
+                        lhsT_scale=scales[:, node_cols],
+                        rhs=w_words[:, 2 * N_BANK * h : 2 * N_BANK * (h + 1)].bitcast(FP4X4),
+                        rhs_scale=w_scales[:, N_BANK * h : N_BANK * (h + 1)],
+                        start=True,
+                        stop=True,
+                    )
+                    out_cols = slice(N_BANK * h, N_BANK * (h + 1))
+                    nc.vector.tensor_tensor(out=rows[:, out_cols], in0=acc[:], in1=bias[:, out_cols], op=ADD)
+                node = P * (chunk_tiles * g + j)
+                nc.sync.dma_start(out=out[i, node : node + P, :], in_=rows[:])
+
+        x_t = elem.tile([P, H + 2, W + 2, PACK], BF16)
+        nc.vector.memset(x_t[:], 0.0)
+        x_t_words = x_t[:].bitcast(F32)
+        for g in range(chunks):
+            words = psum_words.tile([P, 2, chunk_tiles * P], F32)
+            for j in range(chunk_tiles):
+                x_words = x_last[:, chunk_tiles * g + j, :].bitcast(F32)
+                for u in range(2):
+                    nc.tensor.transpose(out=words[:, u, P * j : P * (j + 1)], in_=x_words[:, u::2], identity=ident[:])
+            top = 1 + chunk_rows * g
+            nc.scalar.copy(
+                out=x_t_words[:, top : top + chunk_rows, 1 : W + 1, :],
+                in_=words[:].rearrange("p u (r c) -> p r c u", c=W),
+            )
+
+        sides = elem.tile([P, H, W, PACK], F32)
+        trios = elem.tile([P, H + 2, W, PACK], F32)
+        nc.gpsimd.memset(trios[:, 0, :, :], 0.0)
+        nc.gpsimd.memset(trios[:, H + 1, :, :], 0.0)
+
+        def sum_along_rows(g):
+            top = chunk_rows * g
+            here = x_t[:, 1 + top : 1 + top + chunk_rows, :, :]
+            nc.gpsimd.tensor_tensor(out=sides[:, top : top + chunk_rows, :, :], in0=here[:, :, 0:W, :], in1=here[:, :, 2 : W + 2, :], op=ADD)
+            nc.gpsimd.tensor_tensor(
+                out=trios[:, 1 + top : 1 + top + chunk_rows, :, :],
+                in0=sides[:, top : top + chunk_rows, :, :],
+                in1=here[:, :, 1 : W + 1, :],
+                op=ADD,
+            )
+
+        def sum_across_rows(g):
+            top = chunk_rows * g
+            ring = ring_pool.tile([P, chunk_rows, W, PACK], F32)
+            nc.gpsimd.tensor_tensor(out=ring[:], in0=trios[:, top : top + chunk_rows, :, :], in1=trios[:, top + 2 : top + 2 + chunk_rows, :, :], op=ADD)
+            grouped = late.tile([P, chunk_tiles, P, PACK], BF16, align_bytes=64, name="late_grouped")
+            nc.gpsimd.tensor_tensor(
+                out=grouped[:].rearrange("p j (r c) t -> p (j r) c t", c=W),
+                in0=ring[:],
+                in1=sides[:, top : top + chunk_rows, :, :],
+                op=ADD,
+            )
+            return grouped
+
+        late_grouped = []
+        sum_along_rows(0)
+        for g in range(1, chunks):
+            sum_along_rows(g)
+            late_grouped.append(sum_across_rows(g - 1))
+        late_grouped.append(sum_across_rows(chunks - 1))
+
+        for i in range(tensor_images):
+            for g in range(chunks):
+                grouped = stage.tile([P, chunk_tiles, P, PACK], BF16, align_bytes=64)
+                for j in range(chunk_tiles):
+                    sums = psum_sums.tile([P, PACK, P], F32)
+                    for half in range(2):
+                        d = 2 * (chunk_tiles * g + j) + half
+                        wanted = W * (2 * d - first_row(d))
+                        for t in range(PACK):
+                            nc.tensor.matmul(
+                                out=sums[:, t, half_nodes * half : half_nodes * (half + 1)],
+                                lhsT=x_windows[i][:, d, t::PACK],
+                                rhs=neighbours[:, wanted : wanted + half_nodes],
+                                start=True,
+                                stop=True,
+                            )
+                    nc.scalar.copy(out=grouped[:, j, :, :], in_=sums[:].rearrange("p t n -> p n t"))
+                multiply_and_store(grouped, i, g)
+        for g in range(chunks):
+            multiply_and_store(late_grouped[g], last, g)

@@ -175,6 +175,14 @@ def tile_graphconvlayer_kernel(tc, X, Wm_words, Wm_scales, b, H, W, out):
 
         for i in range(tensor_images):
             for g in range(chunks):
+                pairs = stage.tile([P, chunk_windows, 2, P], F32)
+                nc.scalar.copy(
+                    out=pairs[:],
+                    in_=x_windows[i][:, chunk_windows * g : chunk_windows * (g + 1), :]
+                    .bitcast(F32)
+                    .rearrange("p w (q u) -> p w u q", u=2),
+                )
+                sorted_x = pairs[:].bitcast(BF16)
                 grouped = stage.tile([P, chunk_tiles, P, PACK], BF16, align_bytes=64)
                 for j in range(chunk_tiles):
                     sums = psum_sums.tile([P, PACK, P], F32)
@@ -184,7 +192,7 @@ def tile_graphconvlayer_kernel(tc, X, Wm_words, Wm_scales, b, H, W, out):
                         for t in range(PACK):
                             nc.tensor.matmul(
                                 out=sums[:, t, half_nodes * half : half_nodes * (half + 1)],
-                                lhsT=x_windows[i][:, d, t::PACK],
+                                lhsT=sorted_x[:, d - chunk_windows * g, t // 2, t % 2 :: 2],
                                 rhs=neighbours[:, wanted : wanted + half_nodes],
                                 start=True,
                                 stop=True,

@@ -142,47 +142,41 @@ def tile_graphconvlayer_kernel(tc, X, Wm_words, Wm_scales, b, H, W, out):
         nc.gpsimd.memset(trios[:, 0, :, :], 0.0)
         nc.gpsimd.memset(trios[:, H + 1, :, :], 0.0)
 
-        def sum_along_rows(g):
-            top = chunk_rows * g
-            here = x_t[:, 1 + top : 1 + top + chunk_rows, :, :]
-            nc.gpsimd.tensor_tensor(out=sides[:, top : top + chunk_rows, :, :], in0=here[:, :, 0:W, :], in1=here[:, :, 2 : W + 2, :], op=ADD)
+        def sum_along_rows(s):
+            top = tile_rows * s
+            here = x_t[:, 1 + top : 1 + top + tile_rows, :, :]
+            nc.gpsimd.tensor_tensor(out=sides[:, top : top + tile_rows, :, :], in0=here[:, :, 0:W, :], in1=here[:, :, 2 : W + 2, :], op=ADD)
             nc.gpsimd.tensor_tensor(
-                out=trios[:, 1 + top : 1 + top + chunk_rows, :, :],
-                in0=sides[:, top : top + chunk_rows, :, :],
+                out=trios[:, 1 + top : 1 + top + tile_rows, :, :],
+                in0=sides[:, top : top + tile_rows, :, :],
                 in1=here[:, :, 1 : W + 1, :],
                 op=ADD,
             )
 
-        def sum_across_rows(g):
-            top = chunk_rows * g
-            ring = ring_pool.tile([P, chunk_rows, W, PACK], F32)
-            nc.gpsimd.tensor_tensor(out=ring[:], in0=trios[:, top : top + chunk_rows, :, :], in1=trios[:, top + 2 : top + 2 + chunk_rows, :, :], op=ADD)
-            grouped = late.tile([P, chunk_tiles, P, PACK], BF16, align_bytes=64, name="late_grouped")
+        late_grouped = [
+            late.tile([P, chunk_tiles, P, PACK], BF16, align_bytes=64, name="late_grouped") for g in range(chunks)
+        ]
+
+        def sum_across_rows(s):
+            top = tile_rows * s
+            ring = ring_pool.tile([P, tile_rows, W, PACK], F32)
+            nc.gpsimd.tensor_tensor(out=ring[:], in0=trios[:, top : top + tile_rows, :, :], in1=trios[:, top + 2 : top + 2 + tile_rows, :, :], op=ADD)
             nc.gpsimd.tensor_tensor(
-                out=grouped[:].rearrange("p j (r c) t -> p (j r) c t", c=W),
+                out=late_grouped[s // chunk_tiles][:, s % chunk_tiles, :, :].rearrange("p (r c) t -> p r c t", c=W),
                 in0=ring[:],
-                in1=sides[:, top : top + chunk_rows, :, :],
+                in1=sides[:, top : top + tile_rows, :, :],
                 op=ADD,
             )
-            return grouped
 
-        late_grouped = []
+        strips = H // tile_rows
         sum_along_rows(0)
-        for g in range(1, chunks):
-            sum_along_rows(g)
-            late_grouped.append(sum_across_rows(g - 1))
-        late_grouped.append(sum_across_rows(chunks - 1))
+        for s in range(1, strips):
+            sum_along_rows(s)
+            sum_across_rows(s - 1)
+        sum_across_rows(strips - 1)
 
         for i in range(tensor_images):
             for g in range(chunks):
-                pairs = stage.tile([P, chunk_windows, 2, P], F32)
-                nc.scalar.copy(
-                    out=pairs[:],
-                    in_=x_windows[i][:, chunk_windows * g : chunk_windows * (g + 1), :]
-                    .bitcast(F32)
-                    .rearrange("p w (q u) -> p w u q", u=2),
-                )
-                sorted_x = pairs[:].bitcast(BF16)
                 grouped = stage.tile([P, chunk_tiles, P, PACK], BF16, align_bytes=64)
                 for j in range(chunk_tiles):
                     sums = psum_sums.tile([P, PACK, P], F32)
@@ -192,7 +186,7 @@ def tile_graphconvlayer_kernel(tc, X, Wm_words, Wm_scales, b, H, W, out):
                         for t in range(PACK):
                             nc.tensor.matmul(
                                 out=sums[:, t, half_nodes * half : half_nodes * (half + 1)],
-                                lhsT=sorted_x[:, d - chunk_windows * g, t // 2, t % 2 :: 2],
+                                lhsT=x_windows[i][:, d, t::PACK],
                                 rhs=neighbours[:, wanted : wanted + half_nodes],
                                 start=True,
                                 stop=True,

@@ -16,6 +16,10 @@ P = 128
 PACK = 4
 N_BANK = 512
 
+GROUP_TILES = 4
+LEAD = GROUP_TILES + 1
+VECTOR_TILES = 2
+
 FLOPS = 2 * 4 * 1024 * 512 * 1024
 
 
@@ -25,61 +29,64 @@ def tile_graphconvlayer_kernel(tc, X, Wm_words, Wm_scales, b, H, W, out):
     outputs = out.shape[2]
     assert features == P * PACK and nodes == H * W and P % W == 0
     tile_rows = P // W
+    tiles = nodes // P
     half_nodes = P // 2
-    windows = H // 2
-    chunk_rows = 2 * tile_rows
-    chunk_tiles = 2
-    chunk_windows = 2 * chunk_tiles
-    chunks = H // chunk_rows
-    tensor_images = images - 1
     last = images - 1
+    tensor_tiles = last * tiles
+    all_tiles = images * tiles
 
     with ExitStack() as ctx:
         const = ctx.enter_context(tc.tile_pool(name="const", bufs=1))
         xin = ctx.enter_context(tc.tile_pool(name="xin", bufs=1))
         elem = ctx.enter_context(tc.tile_pool(name="elem", bufs=1))
         ring_pool = ctx.enter_context(tc.tile_pool(name="ring", bufs=2))
-        late = ctx.enter_context(tc.tile_pool(name="late", bufs=chunks))
         stage = ctx.enter_context(tc.tile_pool(name="stage", bufs=3))
-        result = ctx.enter_context(tc.tile_pool(name="result", bufs=10))
+        result = ctx.enter_context(tc.tile_pool(name="result", bufs=12))
         psum_sums = ctx.enter_context(tc.psum_pool(name="psum_sums", bufs=2))
         psum_words = ctx.enter_context(tc.psum_pool(name="psum_words", bufs=2))
         psum_acc = ctx.enter_context(tc.psum_pool(name="psum_acc", bufs=4))
-
-        w_scales = const.tile([P, outputs], U8, align_bytes=64)
-        nc.vector.memset(w_scales[:].bitcast(I32), 0)
-        w_words = const.tile([P, 2 * outputs], U8, align_bytes=64)
+        ctx.enter_context(tc.manual_schedule())
 
         def first_row(d):
             return min(max(2 * d - 1, 0), H - tile_rows)
 
-        x_windows = [xin.tile([P, windows, features], BF16, name="x_image%d" % i) for i in range(tensor_images)]
+        x_windows = [xin.tile([P, 2 * tiles, features], BF16, name="x_image%d" % i) for i in range(last)]
+        x_last = xin.tile([P, tiles, features], BF16)
+        w_words = const.tile([P, 2 * outputs], U8, align_bytes=64)
+        w_scales = const.tile([P, outputs], U8, align_bytes=64)
+        bias = const.tile([P, outputs], BF16)
+        nc.vector.memset(w_scales[:].bitcast(I32), 0)
+        x_t = elem.tile([P, H + 2, W + 2, PACK], BF16)
+        nc.vector.memset(x_t[:], 0.0)
 
-        def load_windows(i, g):
-            for d in range(chunk_windows * g, chunk_windows * (g + 1)):
+        def load_windows(n):
+            i, e = divmod(n, tiles)
+            for d in (2 * e, 2 * e + 1):
                 node = W * first_row(d)
                 nc.sync.dma_start(out=x_windows[i][:, d, :], in_=X[i, node : node + P, :])
 
+        def load_last(e):
+            nc.sync.dma_start(
+                out=x_last[:, e : e + 2, :],
+                in_=X[last, P * e : P * (e + 2), :].rearrange("(j p) f -> p j f", p=P),
+            )
+
+        early = VECTOR_TILES + 2
+        for e in range(0, early, 2):
+            load_last(e)
+        for n in range(LEAD):
+            load_windows(n)
+        nc.sync.dma_start(out=w_words[:].bitcast(I32), in_=Wm_words[0].bitcast(I32))
         for quadrant in range(4):
             nc.sync.dma_start(
                 out=w_scales[32 * quadrant : 32 * quadrant + 4, :].bitcast(I32),
                 in_=Wm_scales[0, 4 * quadrant : 4 * quadrant + 4, :].bitcast(I32),
             )
-        load_windows(0, 0)
-        nc.sync.dma_start(out=w_words[:].bitcast(I32), in_=Wm_words[0].bitcast(I32))
-        bias = const.tile([P, outputs], BF16)
-        nc.scalar.dma_start(out=bias[:], in_=b.partition_broadcast(P))
-        x_last = xin.tile([P, nodes // P, features], BF16)
-        for g in range(chunks):
-            first = chunk_tiles * g
-            nc.sync.dma_start(
-                out=x_last[:, first : first + chunk_tiles, :],
-                in_=X[last, P * first : P * (first + chunk_tiles), :].rearrange("(j p) f -> p j f", p=P),
-            )
-        for i in range(tensor_images):
-            for g in range(chunks):
-                if (i, g) != (0, 0):
-                    load_windows(i, g)
+        nc.sync.dma_start(out=bias[:], in_=b.partition_broadcast(P))
+        for e in range(early, tiles, 2):
+            load_last(e)
+        for n in range(LEAD, tensor_tiles):
+            load_windows(n)
 
         ident = const.tile([P, P], F32)
         make_identity(nc, ident[:])
@@ -95,103 +102,121 @@ def tile_graphconvlayer_kernel(tc, X, Wm_words, Wm_scales, b, H, W, out):
         neighbours = const.tile([P, P], BF16)
         nc.vector.tensor_copy(out=neighbours[:], in_=around[:].rearrange("p r c -> p (r c)"))
 
-        def multiply_and_store(grouped, i, g):
-            codes = stage.tile([P, chunk_tiles * P], U32, align_bytes=64)
-            scales = stage.tile([P, chunk_tiles * P], U8, align_bytes=64)
-            nc.vector.quantize_mx(
-                out=codes[:].bitcast(FP8X4),
-                scales=scales[:],
-                in_=grouped[:].rearrange("p j n t -> p (j n t)"),
-            )
-            for j in range(chunk_tiles):
-                rows = result.tile([P, outputs], F32)
-                node_cols = slice(P * j, P * (j + 1))
-                for h in range(outputs // N_BANK):
-                    acc = psum_acc.tile([P, N_BANK], F32)
-                    nc.tensor.matmul_mx(
-                        out=acc[:],
-                        lhsT=codes[:, node_cols].bitcast(FP8X4),
-                        lhsT_scale=scales[:, node_cols],
-                        rhs=w_words[:, 2 * N_BANK * h : 2 * N_BANK * (h + 1)].bitcast(FP4X4),
-                        rhs_scale=w_scales[:, N_BANK * h : N_BANK * (h + 1)],
-                        start=True,
-                        stop=True,
-                    )
-                    out_cols = slice(N_BANK * h, N_BANK * (h + 1))
-                    nc.vector.tensor_tensor(out=rows[:, out_cols], in0=acc[:], in1=bias[:, out_cols], op=ADD)
-                node = P * (chunk_tiles * g + j)
-                nc.sync.dma_start(out=out[i, node : node + P, :], in_=rows[:])
-
-        x_t = elem.tile([P, H + 2, W + 2, PACK], BF16)
-        nc.vector.memset(x_t[:], 0.0)
         x_t_words = x_t[:].bitcast(F32)
-        for g in range(chunks):
-            words = psum_words.tile([P, 2, chunk_tiles * P], F32)
-            for j in range(chunk_tiles):
-                x_words = x_last[:, chunk_tiles * g + j, :].bitcast(F32)
+
+        def transpose_last(e):
+            words = psum_words.tile([P, 2, 2 * P], F32)
+            for j in range(2):
+                x_words = x_last[:, e + j, :].bitcast(F32)
                 for u in range(2):
                     nc.tensor.transpose(out=words[:, u, P * j : P * (j + 1)], in_=x_words[:, u::2], identity=ident[:])
-            top = 1 + chunk_rows * g
+            top = 1 + tile_rows * e
             nc.scalar.copy(
-                out=x_t_words[:, top : top + chunk_rows, 1 : W + 1, :],
+                out=x_t_words[:, top : top + 2 * tile_rows, 1 : W + 1, :],
                 in_=words[:].rearrange("p u (r c) -> p r c u", c=W),
             )
+
+        grouped = {}
+        for g in range(tensor_tiles // GROUP_TILES, all_tiles // GROUP_TILES):
+            grouped[g] = elem.tile([P, GROUP_TILES, P, PACK], BF16, align_bytes=64, name="late_grouped%d" % g)
 
         sides = elem.tile([P, H, W, PACK], F32)
         trios = elem.tile([P, H + 2, W, PACK], F32)
         nc.gpsimd.memset(trios[:, 0, :, :], 0.0)
         nc.gpsimd.memset(trios[:, H + 1, :, :], 0.0)
 
-        def sum_along_rows(s):
-            top = tile_rows * s
+        def sum_along_rows(engine, e):
+            top = tile_rows * e
             here = x_t[:, 1 + top : 1 + top + tile_rows, :, :]
-            nc.gpsimd.tensor_tensor(out=sides[:, top : top + tile_rows, :, :], in0=here[:, :, 0:W, :], in1=here[:, :, 2 : W + 2, :], op=ADD)
-            nc.gpsimd.tensor_tensor(
+            engine.tensor_tensor(out=sides[:, top : top + tile_rows, :, :], in0=here[:, :, 0:W, :], in1=here[:, :, 2 : W + 2, :], op=ADD)
+            engine.tensor_tensor(
                 out=trios[:, 1 + top : 1 + top + tile_rows, :, :],
                 in0=sides[:, top : top + tile_rows, :, :],
                 in1=here[:, :, 1 : W + 1, :],
                 op=ADD,
             )
 
-        late_grouped = [
-            late.tile([P, chunk_tiles, P, PACK], BF16, align_bytes=64, name="late_grouped") for g in range(chunks)
-        ]
-
-        def sum_across_rows(s):
-            top = tile_rows * s
+        def sum_across_rows(engine, e):
+            top = tile_rows * e
+            n = tensor_tiles + e
             ring = ring_pool.tile([P, tile_rows, W, PACK], F32)
-            nc.gpsimd.tensor_tensor(out=ring[:], in0=trios[:, top : top + tile_rows, :, :], in1=trios[:, top + 2 : top + 2 + tile_rows, :, :], op=ADD)
-            nc.gpsimd.tensor_tensor(
-                out=late_grouped[s // chunk_tiles][:, s % chunk_tiles, :, :].rearrange("p (r c) t -> p r c t", c=W),
+            engine.tensor_tensor(out=ring[:], in0=trios[:, top : top + tile_rows, :, :], in1=trios[:, top + 2 : top + 2 + tile_rows, :, :], op=ADD)
+            engine.tensor_tensor(
+                out=grouped[n // GROUP_TILES][:, n % GROUP_TILES, :, :].rearrange("p (r c) t -> p r c t", c=W),
                 in0=ring[:],
                 in1=sides[:, top : top + tile_rows, :, :],
                 op=ADD,
             )
 
-        strips = H // tile_rows
-        sum_along_rows(0)
-        for s in range(1, strips):
-            sum_along_rows(s)
-            sum_across_rows(s - 1)
-        sum_across_rows(strips - 1)
+        def sum_on_tensor(n):
+            i, e = divmod(n, tiles)
+            if n % GROUP_TILES == 0:
+                grouped[n // GROUP_TILES] = stage.tile([P, GROUP_TILES, P, PACK], BF16, align_bytes=64, name="grouped")
+            sums = psum_sums.tile([P, PACK, P], F32)
+            for half in range(2):
+                d = 2 * e + half
+                wanted = W * (2 * d - first_row(d))
+                for t in range(PACK):
+                    nc.tensor.matmul(
+                        out=sums[:, t, half_nodes * half : half_nodes * (half + 1)],
+                        lhsT=x_windows[i][:, d, t::PACK],
+                        rhs=neighbours[:, wanted : wanted + half_nodes],
+                        start=True,
+                        stop=True,
+                    )
+            nc.scalar.copy(out=grouped[n // GROUP_TILES][:, n % GROUP_TILES, :, :], in_=sums[:].rearrange("p t n -> p n t"))
 
-        for i in range(tensor_images):
-            for g in range(chunks):
-                grouped = stage.tile([P, chunk_tiles, P, PACK], BF16, align_bytes=64)
-                for j in range(chunk_tiles):
-                    sums = psum_sums.tile([P, PACK, P], F32)
-                    for half in range(2):
-                        d = 2 * (chunk_tiles * g + j) + half
-                        wanted = W * (2 * d - first_row(d))
-                        for t in range(PACK):
-                            nc.tensor.matmul(
-                                out=sums[:, t, half_nodes * half : half_nodes * (half + 1)],
-                                lhsT=x_windows[i][:, d, t::PACK],
-                                rhs=neighbours[:, wanted : wanted + half_nodes],
-                                start=True,
-                                stop=True,
-                            )
-                    nc.scalar.copy(out=grouped[:, j, :, :], in_=sums[:].rearrange("p t n -> p n t"))
-                multiply_and_store(grouped, i, g)
-        for g in range(chunks):
-            multiply_and_store(late_grouped[g], last, g)
+        codes = {}
+        scales = {}
+
+        def quantise(g):
+            codes[g] = stage.tile([P, GROUP_TILES * P], U32, align_bytes=64, name="codes")
+            scales[g] = stage.tile([P, GROUP_TILES * P], U8, align_bytes=64, name="scales")
+            nc.vector.quantize_mx(
+                out=codes[g][:].bitcast(FP8X4),
+                scales=scales[g][:],
+                in_=grouped[g][:].rearrange("p j n t -> p (j n t)"),
+            )
+
+        def multiply_and_store(n):
+            g, j = divmod(n, GROUP_TILES)
+            node_cols = slice(P * j, P * (j + 1))
+            rows = result.tile([P, outputs], F32)
+            for h in range(outputs // N_BANK):
+                acc = psum_acc.tile([P, N_BANK], F32)
+                nc.tensor.matmul_mx(
+                    out=acc[:],
+                    lhsT=codes[g][:, node_cols].bitcast(FP8X4),
+                    lhsT_scale=scales[g][:, node_cols],
+                    rhs=w_words[:, 2 * N_BANK * h : 2 * N_BANK * (h + 1)].bitcast(FP4X4),
+                    rhs_scale=w_scales[:, N_BANK * h : N_BANK * (h + 1)],
+                    start=True,
+                    stop=True,
+                )
+                out_cols = slice(N_BANK * h, N_BANK * (h + 1))
+                nc.vector.tensor_tensor(out=rows[:, out_cols], in0=acc[:], in1=bias[:, out_cols], op=ADD)
+            i, e = divmod(n, tiles)
+            nc.sync.dma_start(out=out[i, P * e : P * (e + 1), :], in_=rows[:])
+
+        for e in range(0, early, 2):
+            transpose_last(e)
+        for n in range(LEAD):
+            sum_on_tensor(n)
+        for e in range(early, tiles, 2):
+            transpose_last(e)
+        for e in range(VECTOR_TILES):
+            sum_along_rows(nc.vector, e)
+        sum_along_rows(nc.gpsimd, VECTOR_TILES)
+        for e in range(VECTOR_TILES):
+            sum_across_rows(nc.vector, e)
+        for e in range(VECTOR_TILES + 1, tiles):
+            sum_along_rows(nc.gpsimd, e)
+            sum_across_rows(nc.gpsimd, e - 1)
+        sum_across_rows(nc.gpsimd, tiles - 1)
+        quantise(0)
+        for n in range(all_tiles):
+            if n + LEAD < tensor_tiles:
+                sum_on_tensor(n + LEAD)
+            if (n + 1) % GROUP_TILES == 0 and n + 1 < all_tiles:
+                quantise((n + 1) // GROUP_TILES)
+            multiply_and_store(n)

@@ -40,6 +40,7 @@ def tile_graphconvlayer_kernel(tc, X, Wm_words, Wm_scales, b, H, W, out):
         xin = ctx.enter_context(tc.tile_pool(name="xin", bufs=1))
         elem = ctx.enter_context(tc.tile_pool(name="elem", bufs=1))
         ring_pool = ctx.enter_context(tc.tile_pool(name="ring", bufs=2))
+        sorting = ctx.enter_context(tc.tile_pool(name="sorting", bufs=4))
         stage = ctx.enter_context(tc.tile_pool(name="stage", bufs=3))
         result = ctx.enter_context(tc.tile_pool(name="result", bufs=12))
         psum_sums = ctx.enter_context(tc.psum_pool(name="psum_sums", bufs=2))
@@ -74,7 +75,7 @@ def tile_graphconvlayer_kernel(tc, X, Wm_words, Wm_scales, b, H, W, out):
         early = VECTOR_TILES + 2
         for e in range(0, early, 2):
             load_last(e)
-        for n in range(LEAD):
+        for n in range(LEAD + 1):
             load_windows(n)
         nc.sync.dma_start(out=w_words[:].bitcast(I32), in_=Wm_words[0].bitcast(I32))
         for quadrant in range(4):
@@ -85,7 +86,7 @@ def tile_graphconvlayer_kernel(tc, X, Wm_words, Wm_scales, b, H, W, out):
         nc.sync.dma_start(out=bias[:], in_=b.partition_broadcast(P))
         for e in range(early, tiles, 2):
             load_last(e)
-        for n in range(LEAD, tensor_tiles):
+        for n in range(LEAD + 1, tensor_tiles):
             load_windows(n)
 
         ident = const.tile([P, P], F32)
@@ -148,8 +149,19 @@ def tile_graphconvlayer_kernel(tc, X, Wm_words, Wm_scales, b, H, W, out):
                 op=ADD,
             )
 
+        pairs = {}
+
+        def sort_words(n):
+            i, e = divmod(n, tiles)
+            pairs[n] = sorting.tile([P, 2, 2, P], F32, name="pairs")
+            nc.scalar.copy(
+                out=pairs[n][:],
+                in_=x_windows[i][:, 2 * e : 2 * e + 2, :].bitcast(F32).rearrange("p w (q u) -> p w u q", u=2),
+            )
+
         def sum_on_tensor(n):
             i, e = divmod(n, tiles)
+            sorted_x = pairs[n][:].bitcast(BF16)
             if n % GROUP_TILES == 0:
                 grouped[n // GROUP_TILES] = stage.tile([P, GROUP_TILES, P, PACK], BF16, align_bytes=64, name="grouped")
             sums = psum_sums.tile([P, PACK, P], F32)
@@ -159,7 +171,7 @@ def tile_graphconvlayer_kernel(tc, X, Wm_words, Wm_scales, b, H, W, out):
                 for t in range(PACK):
                     nc.tensor.matmul(
                         out=sums[:, t, half_nodes * half : half_nodes * (half + 1)],
-                        lhsT=x_windows[i][:, d, t::PACK],
+                        lhsT=sorted_x[:, half, t // 2, t % 2 :: 2],
                         rhs=neighbours[:, wanted : wanted + half_nodes],
                         start=True,
                         stop=True,
@@ -178,12 +190,12 @@ def tile_graphconvlayer_kernel(tc, X, Wm_words, Wm_scales, b, H, W, out):
                 in_=grouped[g][:].rearrange("p j n t -> p (j n t)"),
             )
 
-        def multiply_and_store(n):
+        def multiply(n):
             g, j = divmod(n, GROUP_TILES)
             node_cols = slice(P * j, P * (j + 1))
-            rows = result.tile([P, outputs], F32)
+            banks = []
             for h in range(outputs // N_BANK):
-                acc = psum_acc.tile([P, N_BANK], F32)
+                acc = psum_acc.tile([P, N_BANK], F32, name="acc")
                 nc.tensor.matmul_mx(
                     out=acc[:],
                     lhsT=codes[g][:, node_cols].bitcast(FP8X4),
@@ -193,6 +205,12 @@ def tile_graphconvlayer_kernel(tc, X, Wm_words, Wm_scales, b, H, W, out):
                     start=True,
                     stop=True,
                 )
+                banks.append(acc)
+            return banks
+
+        def add_bias_and_store(n, banks):
+            rows = result.tile([P, outputs], F32)
+            for h, acc in enumerate(banks):
                 out_cols = slice(N_BANK * h, N_BANK * (h + 1))
                 nc.vector.tensor_tensor(out=rows[:, out_cols], in0=acc[:], in1=bias[:, out_cols], op=ADD)
             i, e = divmod(n, tiles)
@@ -200,7 +218,9 @@ def tile_graphconvlayer_kernel(tc, X, Wm_words, Wm_scales, b, H, W, out):
 
         for e in range(0, early, 2):
             transpose_last(e)
+        sort_words(0)
         for n in range(LEAD):
+            sort_words(n + 1)
             sum_on_tensor(n)
         for e in range(early, tiles, 2):
             transpose_last(e)
@@ -215,8 +235,11 @@ def tile_graphconvlayer_kernel(tc, X, Wm_words, Wm_scales, b, H, W, out):
         sum_across_rows(nc.gpsimd, tiles - 1)
         quantise(0)
         for n in range(all_tiles):
+            banks = multiply(n)
+            if n + LEAD + 1 < tensor_tiles:
+                sort_words(n + LEAD + 1)
             if n + LEAD < tensor_tiles:
                 sum_on_tensor(n + LEAD)
             if (n + 1) % GROUP_TILES == 0 and n + 1 < all_tiles:
                 quantise((n + 1) // GROUP_TILES)
-            multiply_and_store(n)
+            add_bias_and_store(n, banks)

@@ -40,7 +40,6 @@ def tile_graphconvlayer_kernel(tc, X, Wm_words, Wm_scales, b, H, W, out):
         xin = ctx.enter_context(tc.tile_pool(name="xin", bufs=1))
         elem = ctx.enter_context(tc.tile_pool(name="elem", bufs=1))
         ring_pool = ctx.enter_context(tc.tile_pool(name="ring", bufs=2))
-        sorting = ctx.enter_context(tc.tile_pool(name="sorting", bufs=4))
         stage = ctx.enter_context(tc.tile_pool(name="stage", bufs=3))
         result = ctx.enter_context(tc.tile_pool(name="result", bufs=12))
         psum_sums = ctx.enter_context(tc.psum_pool(name="psum_sums", bufs=2))
@@ -55,7 +54,8 @@ def tile_graphconvlayer_kernel(tc, X, Wm_words, Wm_scales, b, H, W, out):
         x_last = xin.tile([P, tiles, features], BF16)
         w_words = const.tile([P, 2 * outputs], U8, align_bytes=64)
         w_scales = const.tile([P, outputs], U8, align_bytes=64)
-        bias = const.tile([P, outputs], BF16)
+        b_rows = const.tile([P, P], BF16)
+        nc.vector.memset(b_rows[:], 0.0)
         nc.vector.memset(w_scales[:].bitcast(I32), 0)
         x_t = elem.tile([P, H + 2, W + 2, PACK], BF16)
         nc.vector.memset(x_t[:], 0.0)
@@ -75,7 +75,8 @@ def tile_graphconvlayer_kernel(tc, X, Wm_words, Wm_scales, b, H, W, out):
         early = VECTOR_TILES + 2
         for e in range(0, early, 2):
             load_last(e)
-        for n in range(LEAD + 1):
+        nc.sync.dma_start(out=b_rows[0 : outputs // P, :], in_=b.rearrange("(m n) -> m n", n=P))
+        for n in range(LEAD):
             load_windows(n)
         nc.sync.dma_start(out=w_words[:].bitcast(I32), in_=Wm_words[0].bitcast(I32))
         for quadrant in range(4):
@@ -83,10 +84,9 @@ def tile_graphconvlayer_kernel(tc, X, Wm_words, Wm_scales, b, H, W, out):
                 out=w_scales[32 * quadrant : 32 * quadrant + 4, :].bitcast(I32),
                 in_=Wm_scales[0, 4 * quadrant : 4 * quadrant + 4, :].bitcast(I32),
             )
-        nc.sync.dma_start(out=bias[:], in_=b.partition_broadcast(P))
         for e in range(early, tiles, 2):
             load_last(e)
-        for n in range(LEAD + 1, tensor_tiles):
+        for n in range(LEAD, tensor_tiles):
             load_windows(n)
 
         ident = const.tile([P, P], F32)
@@ -103,10 +103,30 @@ def tile_graphconvlayer_kernel(tc, X, Wm_words, Wm_scales, b, H, W, out):
         neighbours = const.tile([P, P], BF16)
         nc.vector.tensor_copy(out=neighbours[:], in_=around[:].rearrange("p r c -> p (r c)"))
 
+        ident_bf16 = const.tile([P, P], BF16)
+        nc.vector.tensor_copy(out=ident_bf16[:], in_=ident[:])
+        b_cols = const.tile([P, outputs // P], BF16)
+        bias = const.tile([P, outputs], BF16)
+
+        def turn_bias():
+            turned = psum_words.tile([P, P], BF16, tag="words", name="turned")
+            nc.tensor.transpose(out=turned[:], in_=b_rows[:], identity=ident_bf16[:])
+            nc.scalar.copy(out=b_cols[:], in_=turned[:, 0 : outputs // P])
+
+        def spread_bias():
+            spread = psum_words.tile([P, outputs], BF16, tag="words", name="spread")
+            for m in range(outputs // P):
+                nc.tensor.transpose(
+                    out=spread[:, P * m : P * (m + 1)],
+                    in_=b_cols[:, m : m + 1].to_broadcast([P, P]),
+                    identity=ident_bf16[:],
+                )
+            nc.scalar.copy(out=bias[:], in_=spread[:])
+
         x_t_words = x_t[:].bitcast(F32)
 
         def transpose_last(e):
-            words = psum_words.tile([P, 2, 2 * P], F32)
+            words = psum_words.tile([P, 2, 2 * P], F32, tag="words", name="words")
             for j in range(2):
                 x_words = x_last[:, e + j, :].bitcast(F32)
                 for u in range(2):
@@ -149,19 +169,8 @@ def tile_graphconvlayer_kernel(tc, X, Wm_words, Wm_scales, b, H, W, out):
                 op=ADD,
             )
 
-        pairs = {}
-
-        def sort_words(n):
-            i, e = divmod(n, tiles)
-            pairs[n] = sorting.tile([P, 2, 2, P], F32, name="pairs")
-            nc.scalar.copy(
-                out=pairs[n][:],
-                in_=x_windows[i][:, 2 * e : 2 * e + 2, :].bitcast(F32).rearrange("p w (q u) -> p w u q", u=2),
-            )
-
         def sum_on_tensor(n):
             i, e = divmod(n, tiles)
-            sorted_x = pairs[n][:].bitcast(BF16)
             if n % GROUP_TILES == 0:
                 grouped[n // GROUP_TILES] = stage.tile([P, GROUP_TILES, P, PACK], BF16, align_bytes=64, name="grouped")
             sums = psum_sums.tile([P, PACK, P], F32)
@@ -171,7 +180,7 @@ def tile_graphconvlayer_kernel(tc, X, Wm_words, Wm_scales, b, H, W, out):
                 for t in range(PACK):
                     nc.tensor.matmul(
                         out=sums[:, t, half_nodes * half : half_nodes * (half + 1)],
-                        lhsT=sorted_x[:, half, t // 2, t % 2 :: 2],
+                        lhsT=x_windows[i][:, d, t::PACK],
                         rhs=neighbours[:, wanted : wanted + half_nodes],
                         start=True,
                         stop=True,
@@ -218,10 +227,10 @@ def tile_graphconvlayer_kernel(tc, X, Wm_words, Wm_scales, b, H, W, out):
 
         for e in range(0, early, 2):
             transpose_last(e)
-        sort_words(0)
+        turn_bias()
         for n in range(LEAD):
-            sort_words(n + 1)
             sum_on_tensor(n)
+        spread_bias()
         for e in range(early, tiles, 2):
             transpose_last(e)
         for e in range(VECTOR_TILES):
@@ -236,8 +245,6 @@ def tile_graphconvlayer_kernel(tc, X, Wm_words, Wm_scales, b, H, W, out):
         quantise(0)
         for n in range(all_tiles):
             banks = multiply(n)
-            if n + LEAD + 1 < tensor_tiles:
-                sort_words(n + LEAD + 1)
             if n + LEAD < tensor_tiles:
                 sum_on_tensor(n + LEAD)
             if (n + 1) % GROUP_TILES == 0 and n + 1 < all_tiles:

@@ -17,8 +17,8 @@ PACK = 4
 N_BANK = 512
 
 GROUP_TILES = 4
+FIRST_GROUPS = (1, 1, 2)
 LEAD = GROUP_TILES + 1
-VECTOR_TILES = 2
 
 FLOPS = 2 * 4 * 1024 * 512 * 1024
 
@@ -31,34 +31,49 @@ def tile_graphconvlayer_kernel(tc, X, Wm_words, Wm_scales, b, H, W, out):
     tile_rows = P // W
     tiles = nodes // P
     half_nodes = P // 2
-    last = images - 1
-    tensor_tiles = last * tiles
     all_tiles = images * tiles
+    tensor_tiles = all_tiles * outputs // P // 10
+    last = images - 1
+    first_elem = tensor_tiles - last * tiles
+    assert tensor_tiles == 25 and 0 < first_elem < tiles
+
+    group_sizes = list(FIRST_GROUPS) + [GROUP_TILES] * ((all_tiles - sum(FIRST_GROUPS)) // GROUP_TILES)
+    first_tile = [sum(group_sizes[:g]) for g in range(len(group_sizes))]
+    group_of = [g for g, size in enumerate(group_sizes) for j in range(size)]
+    place_of = [j for size in group_sizes for j in range(size)]
+    assert len(group_of) == all_tiles
 
     with ExitStack() as ctx:
         const = ctx.enter_context(tc.tile_pool(name="const", bufs=1))
         xin = ctx.enter_context(tc.tile_pool(name="xin", bufs=1))
         elem = ctx.enter_context(tc.tile_pool(name="elem", bufs=1))
         ring_pool = ctx.enter_context(tc.tile_pool(name="ring", bufs=2))
-        stage = ctx.enter_context(tc.tile_pool(name="stage", bufs=3))
+        stage = ctx.enter_context(tc.tile_pool(name="stage", bufs=4))
         result = ctx.enter_context(tc.tile_pool(name="result", bufs=12))
         psum_sums = ctx.enter_context(tc.psum_pool(name="psum_sums", bufs=2))
         psum_words = ctx.enter_context(tc.psum_pool(name="psum_words", bufs=2))
         psum_acc = ctx.enter_context(tc.psum_pool(name="psum_acc", bufs=4))
         ctx.enter_context(tc.manual_schedule())
 
+        warm = const.tile([P, 2], F32)
+        nc.gpsimd.memset(warm[:, 0:1], 0.0)
+        nc.scalar.copy(out=warm[:, 1:2], in_=warm[:, 0:1])
+
         def first_row(d):
             return min(max(2 * d - 1, 0), H - tile_rows)
 
-        x_windows = [xin.tile([P, 2 * tiles, features], BF16, name="x_image%d" % i) for i in range(last)]
+        x_windows = [
+            xin.tile([P, 2 * min(tiles, tensor_tiles - tiles * i), features], BF16, name="x_image%d" % i) for i in range(images)
+        ]
         x_last = xin.tile([P, tiles, features], BF16)
         w_words = const.tile([P, 2 * outputs], U8, align_bytes=64)
         w_scales = const.tile([P, outputs], U8, align_bytes=64)
         b_rows = const.tile([P, P], BF16)
         nc.vector.memset(b_rows[:], 0.0)
         nc.vector.memset(w_scales[:].bitcast(I32), 0)
-        x_t = elem.tile([P, H + 2, W + 2, PACK], BF16)
-        nc.vector.memset(x_t[:], 0.0)
+        x_t = elem.tile([P, H, W + 2, PACK], BF16)
+        nc.gpsimd.memset(x_t[:, :, 0, :], 0.0)
+        nc.gpsimd.memset(x_t[:, :, W + 1, :], 0.0)
 
         def load_windows(n):
             i, e = divmod(n, tiles)
@@ -72,22 +87,21 @@ def tile_graphconvlayer_kernel(tc, X, Wm_words, Wm_scales, b, H, W, out):
                 in_=X[last, P * e : P * (e + 2), :].rearrange("(j p) f -> p j f", p=P),
             )
 
-        early = VECTOR_TILES + 2
-        for e in range(0, early, 2):
-            load_last(e)
+        def load_weight():
+            nc.sync.dma_start(out=w_words[:].bitcast(I32), in_=Wm_words[0].bitcast(I32))
+            for quadrant in range(4):
+                nc.sync.dma_start(
+                    out=w_scales[32 * quadrant : 32 * quadrant + 4, :].bitcast(I32),
+                    in_=Wm_scales[0, 4 * quadrant : 4 * quadrant + 4, :].bitcast(I32),
+                )
+
         nc.sync.dma_start(out=b_rows[0 : outputs // P, :], in_=b.rearrange("(m n) -> m n", n=P))
-        for n in range(LEAD):
+        for n in range(tensor_tiles):
+            if n % 2 == 0 and n < tiles:
+                load_last(n)
             load_windows(n)
-        nc.sync.dma_start(out=w_words[:].bitcast(I32), in_=Wm_words[0].bitcast(I32))
-        for quadrant in range(4):
-            nc.sync.dma_start(
-                out=w_scales[32 * quadrant : 32 * quadrant + 4, :].bitcast(I32),
-                in_=Wm_scales[0, 4 * quadrant : 4 * quadrant + 4, :].bitcast(I32),
-            )
-        for e in range(early, tiles, 2):
-            load_last(e)
-        for n in range(LEAD, tensor_tiles):
-            load_windows(n)
+            if n == 1:
+                load_weight()
 
         ident = const.tile([P, P], F32)
         make_identity(nc, ident[:])
@@ -111,7 +125,7 @@ def tile_graphconvlayer_kernel(tc, X, Wm_words, Wm_scales, b, H, W, out):
         def turn_bias():
             turned = psum_words.tile([P, P], BF16, tag="words", name="turned")
             nc.tensor.transpose(out=turned[:], in_=b_rows[:], identity=ident_bf16[:])
-            nc.scalar.copy(out=b_cols[:], in_=turned[:, 0 : outputs // P])
+            nc.vector.tensor_copy(out=b_cols[:], in_=turned[:, 0 : outputs // P])
 
         def spread_bias():
             spread = psum_words.tile([P, outputs], BF16, tag="words", name="spread")
@@ -121,7 +135,7 @@ def tile_graphconvlayer_kernel(tc, X, Wm_words, Wm_scales, b, H, W, out):
                     in_=b_cols[:, m : m + 1].to_broadcast([P, P]),
                     identity=ident_bf16[:],
                 )
-            nc.scalar.copy(out=bias[:], in_=spread[:])
+            nc.vector.tensor_copy(out=bias[:], in_=spread[:])
 
         x_t_words = x_t[:].bitcast(F32)
 
@@ -131,48 +145,58 @@ def tile_graphconvlayer_kernel(tc, X, Wm_words, Wm_scales, b, H, W, out):
                 x_words = x_last[:, e + j, :].bitcast(F32)
                 for u in range(2):
                     nc.tensor.transpose(out=words[:, u, P * j : P * (j + 1)], in_=x_words[:, u::2], identity=ident[:])
-            top = 1 + tile_rows * e
+            top = tile_rows * e
             nc.scalar.copy(
                 out=x_t_words[:, top : top + 2 * tile_rows, 1 : W + 1, :],
                 in_=words[:].rearrange("p u (r c) -> p r c u", c=W),
             )
 
         grouped = {}
-        for g in range(tensor_tiles // GROUP_TILES, all_tiles // GROUP_TILES):
-            grouped[g] = elem.tile([P, GROUP_TILES, P, PACK], BF16, align_bytes=64, name="late_grouped%d" % g)
+        for g in range(group_of[tensor_tiles], len(group_sizes)):
+            grouped[g] = elem.tile([P, group_sizes[g], P, PACK], BF16, align_bytes=64, name="late_grouped%d" % g)
 
         sides = elem.tile([P, H, W, PACK], F32)
-        trios = elem.tile([P, H + 2, W, PACK], F32)
-        nc.gpsimd.memset(trios[:, 0, :, :], 0.0)
-        nc.gpsimd.memset(trios[:, H + 1, :, :], 0.0)
+        trios = elem.tile([P, H + 1, W, PACK], F32)
+        nc.gpsimd.memset(trios[:, H, :, :], 0.0)
 
-        def sum_along_rows(engine, e):
-            top = tile_rows * e
-            here = x_t[:, 1 + top : 1 + top + tile_rows, :, :]
-            engine.tensor_tensor(out=sides[:, top : top + tile_rows, :, :], in0=here[:, :, 0:W, :], in1=here[:, :, 2 : W + 2, :], op=ADD)
-            engine.tensor_tensor(
-                out=trios[:, 1 + top : 1 + top + tile_rows, :, :],
-                in0=sides[:, top : top + tile_rows, :, :],
+        def sum_along_rows(top, rows):
+            here = x_t[:, top : top + rows, :, :]
+            nc.gpsimd.tensor_tensor(out=sides[:, top : top + rows, :, :], in0=here[:, :, 0:W, :], in1=here[:, :, 2 : W + 2, :], op=ADD)
+            nc.gpsimd.tensor_tensor(
+                out=trios[:, top : top + rows, :, :],
+                in0=sides[:, top : top + rows, :, :],
                 in1=here[:, :, 1 : W + 1, :],
                 op=ADD,
             )
 
-        def sum_across_rows(engine, e):
+        def sum_across_rows(e):
             top = tile_rows * e
-            n = tensor_tiles + e
+            n = last * tiles + e
             ring = ring_pool.tile([P, tile_rows, W, PACK], F32)
-            engine.tensor_tensor(out=ring[:], in0=trios[:, top : top + tile_rows, :, :], in1=trios[:, top + 2 : top + 2 + tile_rows, :, :], op=ADD)
-            engine.tensor_tensor(
-                out=grouped[n // GROUP_TILES][:, n % GROUP_TILES, :, :].rearrange("p (r c) t -> p r c t", c=W),
+            nc.gpsimd.tensor_tensor(out=ring[:], in0=trios[:, top - 1 : top - 1 + tile_rows, :, :], in1=trios[:, top + 1 : top + 1 + tile_rows, :, :], op=ADD)
+            nc.gpsimd.tensor_tensor(
+                out=grouped[group_of[n]][:, place_of[n], :, :].rearrange("p (r c) t -> p r c t", c=W),
                 in0=ring[:],
                 in1=sides[:, top : top + tile_rows, :, :],
                 op=ADD,
             )
 
+        def sum_elementwise(e):
+            for f in (e, e + 1):
+                if f == first_elem - 1:
+                    sum_along_rows(tile_rows * f + tile_rows - 1, 1)
+                if f >= first_elem:
+                    sum_along_rows(tile_rows * f, tile_rows)
+                if f > first_elem:
+                    sum_across_rows(f - 1)
+            if e + 2 == tiles:
+                sum_across_rows(tiles - 1)
+
         def sum_on_tensor(n):
             i, e = divmod(n, tiles)
-            if n % GROUP_TILES == 0:
-                grouped[n // GROUP_TILES] = stage.tile([P, GROUP_TILES, P, PACK], BF16, align_bytes=64, name="grouped")
+            g = group_of[n]
+            if g not in grouped:
+                grouped[g] = stage.tile([P, group_sizes[g], P, PACK], BF16, align_bytes=64, name="grouped")
             sums = psum_sums.tile([P, PACK, P], F32)
             for half in range(2):
                 d = 2 * e + half
@@ -185,14 +209,14 @@ def tile_graphconvlayer_kernel(tc, X, Wm_words, Wm_scales, b, H, W, out):
                         start=True,
                         stop=True,
                     )
-            nc.scalar.copy(out=grouped[n // GROUP_TILES][:, n % GROUP_TILES, :, :], in_=sums[:].rearrange("p t n -> p n t"))
+            nc.scalar.copy(out=grouped[g][:, place_of[n], :, :], in_=sums[:].rearrange("p t n -> p n t"))
 
         codes = {}
         scales = {}
 
         def quantise(g):
-            codes[g] = stage.tile([P, GROUP_TILES * P], U32, align_bytes=64, name="codes")
-            scales[g] = stage.tile([P, GROUP_TILES * P], U8, align_bytes=64, name="scales")
+            codes[g] = stage.tile([P, group_sizes[g] * P], U32, align_bytes=64, name="codes")
+            scales[g] = stage.tile([P, group_sizes[g] * P], U8, align_bytes=64, name="scales")
             nc.vector.quantize_mx(
                 out=codes[g][:].bitcast(FP8X4),
                 scales=scales[g][:],
@@ -200,7 +224,7 @@ def tile_graphconvlayer_kernel(tc, X, Wm_words, Wm_scales, b, H, W, out):
             )
 
         def multiply(n):
-            g, j = divmod(n, GROUP_TILES)
+            g, j = group_of[n], place_of[n]
             node_cols = slice(P * j, P * (j + 1))
             banks = []
             for h in range(outputs // N_BANK):
@@ -225,28 +249,25 @@ def tile_graphconvlayer_kernel(tc, X, Wm_words, Wm_scales, b, H, W, out):
             i, e = divmod(n, tiles)
             nc.sync.dma_start(out=out[i, P * e : P * (e + 1), :], in_=rows[:])
 
-        for e in range(0, early, 2):
-            transpose_last(e)
+        def summed_by(n):
+            return min(2 * n + 4, n + LEAD + 1, tensor_tiles)
+
+        transpose_last(0)
+        sum_elementwise(0)
         turn_bias()
-        for n in range(LEAD):
-            sum_on_tensor(n)
         spread_bias()
-        for e in range(early, tiles, 2):
-            transpose_last(e)
-        for e in range(VECTOR_TILES):
-            sum_along_rows(nc.vector, e)
-        sum_along_rows(nc.gpsimd, VECTOR_TILES)
-        for e in range(VECTOR_TILES):
-            sum_across_rows(nc.vector, e)
-        for e in range(VECTOR_TILES + 1, tiles):
-            sum_along_rows(nc.gpsimd, e)
-            sum_across_rows(nc.gpsimd, e - 1)
-        sum_across_rows(nc.gpsimd, tiles - 1)
+        for k in range(summed_by(-1)):
+            sum_on_tensor(k)
+        transpose_last(2)
+        sum_elementwise(2)
         quantise(0)
         for n in range(all_tiles):
             banks = multiply(n)
-            if n + LEAD < tensor_tiles:
-                sum_on_tensor(n + LEAD)
-            if (n + 1) % GROUP_TILES == 0 and n + 1 < all_tiles:
-                quantise((n + 1) // GROUP_TILES)
+            for k in range(summed_by(n - 1), summed_by(n)):
+                sum_on_tensor(k)
+            if n % 2 == 0 and 4 <= n + 2 < tiles:
+                transpose_last(n + 2)
+                sum_elementwise(n + 2)
+            if n + 1 in first_tile:
+                quantise(group_of[n + 1])
             add_bias_and_store(n, banks)

from contextlib import ExitStack

import concourse.mybir as mybir
from concourse.masks import make_identity

F32 = mybir.dt.float32
BF16 = mybir.dt.bfloat16
I32 = mybir.dt.int32
U32 = mybir.dt.uint32
U8 = mybir.dt.uint8
FP8X4 = mybir.dt.float8_e4m3fn_x4
FP4X4 = mybir.dt.float4_e2m1fn_x4
ADD = mybir.AluOpType.add

P = 128
PACK = 4
N_BANK = 512

GROUP_TILES = 4
FIRST_GROUPS = (1, 1, 2)
LEAD = GROUP_TILES + 1

FLOPS = 2 * 4 * 1024 * 512 * 1024


def tile_graphconvlayer_kernel(tc, X, Wm_words, Wm_scales, b, H, W, out):
    nc = tc.nc
    images, nodes, features = X.shape
    outputs = out.shape[2]
    assert features == P * PACK and nodes == H * W and P % W == 0
    tile_rows = P // W
    tiles = nodes // P
    half_nodes = P // 2
    all_tiles = images * tiles
    tensor_tiles = all_tiles * outputs // P // 10
    last = images - 1
    first_elem = tensor_tiles - last * tiles
    assert tensor_tiles == 25 and 0 < first_elem < tiles

    group_sizes = list(FIRST_GROUPS) + [GROUP_TILES] * ((all_tiles - sum(FIRST_GROUPS)) // GROUP_TILES)
    first_tile = [sum(group_sizes[:g]) for g in range(len(group_sizes))]
    group_of = [g for g, size in enumerate(group_sizes) for j in range(size)]
    place_of = [j for size in group_sizes for j in range(size)]
    assert len(group_of) == all_tiles

    with ExitStack() as ctx:
        const = ctx.enter_context(tc.tile_pool(name="const", bufs=1))
        xin = ctx.enter_context(tc.tile_pool(name="xin", bufs=1))
        elem = ctx.enter_context(tc.tile_pool(name="elem", bufs=1))
        ring_pool = ctx.enter_context(tc.tile_pool(name="ring", bufs=2))
        stage = ctx.enter_context(tc.tile_pool(name="stage", bufs=4))
        result = ctx.enter_context(tc.tile_pool(name="result", bufs=12))
        psum_sums = ctx.enter_context(tc.psum_pool(name="psum_sums", bufs=2))
        psum_words = ctx.enter_context(tc.psum_pool(name="psum_words", bufs=2))
        psum_acc = ctx.enter_context(tc.psum_pool(name="psum_acc", bufs=4))
        ctx.enter_context(tc.manual_schedule())

        warm = const.tile([P, 2], F32)
        nc.gpsimd.memset(warm[:, 0:1], 0.0)
        nc.scalar.copy(out=warm[:, 1:2], in_=warm[:, 0:1])

        def first_row(d):
            return min(max(2 * d - 1, 0), H - tile_rows)

        x_windows = [
            xin.tile([P, 2 * min(tiles, tensor_tiles - tiles * i), features], BF16, name="x_image%d" % i) for i in range(images)
        ]
        x_last = xin.tile([P, tiles, features], BF16)
        w_words = const.tile([P, 2 * outputs], U8, align_bytes=64)
        w_scales = const.tile([P, outputs], U8, align_bytes=64)
        b_rows = const.tile([P, P], BF16)
        nc.vector.memset(b_rows[:], 0.0)
        nc.vector.memset(w_scales[:].bitcast(I32), 0)
        x_t = elem.tile([P, H, W + 2, PACK], BF16)
        nc.gpsimd.memset(x_t[:, :, 0, :], 0.0)
        nc.gpsimd.memset(x_t[:, :, W + 1, :], 0.0)

        def load_windows(n):
            i, e = divmod(n, tiles)
            for d in (2 * e, 2 * e + 1):
                node = W * first_row(d)
                nc.sync.dma_start(out=x_windows[i][:, d, :], in_=X[i, node : node + P, :])

        def load_last(e):
            nc.sync.dma_start(
                out=x_last[:, e : e + 2, :],
                in_=X[last, P * e : P * (e + 2), :].rearrange("(j p) f -> p j f", p=P),
            )

        def load_weight():
            nc.sync.dma_start(out=w_words[:].bitcast(I32), in_=Wm_words[0].bitcast(I32))
            for quadrant in range(4):
                nc.sync.dma_start(
                    out=w_scales[32 * quadrant : 32 * quadrant + 4, :].bitcast(I32),
                    in_=Wm_scales[0, 4 * quadrant : 4 * quadrant + 4, :].bitcast(I32),
                )

        nc.sync.dma_start(out=b_rows[0 : outputs // P, :], in_=b.rearrange("(m n) -> m n", n=P))
        for n in range(tensor_tiles):
            if n % 2 == 0 and n < tiles:
                load_last(n)
            load_windows(n)
            if n == 1:
                load_weight()

        ident = const.tile([P, P], F32)
        make_identity(nc, ident[:])
        ident_grid = ident[:].rearrange("p (r c) -> p r c", c=W)
        same_row = const.tile([P, tile_rows, W], F32)
        nc.vector.tensor_copy(out=same_row[:], in_=ident_grid)
        nc.vector.tensor_add(out=same_row[:, :, 1:W], in0=same_row[:, :, 1:W], in1=ident_grid[:, :, 0 : W - 1])
        nc.vector.tensor_add(out=same_row[:, :, 0 : W - 1], in0=same_row[:, :, 0 : W - 1], in1=ident_grid[:, :, 1:W])
        around = const.tile([P, tile_rows, W], F32)
        nc.vector.tensor_sub(out=around[:], in0=same_row[:], in1=ident_grid)
        nc.vector.tensor_add(out=around[:, 1:tile_rows, :], in0=around[:, 1:tile_rows, :], in1=same_row[:, 0 : tile_rows - 1, :])
        nc.vector.tensor_add(out=around[:, 0 : tile_rows - 1, :], in0=around[:, 0 : tile_rows - 1, :], in1=same_row[:, 1:tile_rows, :])
        neighbours = const.tile([P, P], BF16)
        nc.vector.tensor_copy(out=neighbours[:], in_=around[:].rearrange("p r c -> p (r c)"))

        ident_bf16 = const.tile([P, P], BF16)
        nc.vector.tensor_copy(out=ident_bf16[:], in_=ident[:])
        b_cols = const.tile([P, outputs // P], BF16)
        bias = const.tile([P, outputs], BF16)

        def turn_bias():
            turned = psum_words.tile([P, P], BF16, tag="words", name="turned")
            nc.tensor.transpose(out=turned[:], in_=b_rows[:], identity=ident_bf16[:])
            nc.vector.tensor_copy(out=b_cols[:], in_=turned[:, 0 : outputs // P])

        def spread_bias():
            spread = psum_words.tile([P, outputs], BF16, tag="words", name="spread")
            for m in range(outputs // P):
                nc.tensor.transpose(
                    out=spread[:, P * m : P * (m + 1)],
                    in_=b_cols[:, m : m + 1].to_broadcast([P, P]),
                    identity=ident_bf16[:],
                )
            nc.vector.tensor_copy(out=bias[:], in_=spread[:])

        x_t_words = x_t[:].bitcast(F32)

        def transpose_last(e):
            words = psum_words.tile([P, 2, 2 * P], F32, tag="words", name="words")
            for j in range(2):
                x_words = x_last[:, e + j, :].bitcast(F32)
                for u in range(2):
                    nc.tensor.transpose(out=words[:, u, P * j : P * (j + 1)], in_=x_words[:, u::2], identity=ident[:])
            top = tile_rows * e
            nc.scalar.copy(
                out=x_t_words[:, top : top + 2 * tile_rows, 1 : W + 1, :],
                in_=words[:].rearrange("p u (r c) -> p r c u", c=W),
            )

        grouped = {}
        for g in range(group_of[tensor_tiles], len(group_sizes)):
            grouped[g] = elem.tile([P, group_sizes[g], P, PACK], BF16, align_bytes=64, name="late_grouped%d" % g)

        sides = elem.tile([P, H, W, PACK], F32)
        trios = elem.tile([P, H + 1, W, PACK], F32)
        nc.gpsimd.memset(trios[:, H, :, :], 0.0)

        def sum_along_rows(top, rows):
            here = x_t[:, top : top + rows, :, :]
            nc.gpsimd.tensor_tensor(out=sides[:, top : top + rows, :, :], in0=here[:, :, 0:W, :], in1=here[:, :, 2 : W + 2, :], op=ADD)
            nc.gpsimd.tensor_tensor(
                out=trios[:, top : top + rows, :, :],
                in0=sides[:, top : top + rows, :, :],
                in1=here[:, :, 1 : W + 1, :],
                op=ADD,
            )

        def sum_across_rows(e):
            top = tile_rows * e
            n = last * tiles + e
            ring = ring_pool.tile([P, tile_rows, W, PACK], F32)
            nc.gpsimd.tensor_tensor(out=ring[:], in0=trios[:, top - 1 : top - 1 + tile_rows, :, :], in1=trios[:, top + 1 : top + 1 + tile_rows, :, :], op=ADD)
            nc.gpsimd.tensor_tensor(
                out=grouped[group_of[n]][:, place_of[n], :, :].rearrange("p (r c) t -> p r c t", c=W),
                in0=ring[:],
                in1=sides[:, top : top + tile_rows, :, :],
                op=ADD,
            )

        def sum_elementwise(e):
            for f in (e, e + 1):
                if f == first_elem - 1:
                    sum_along_rows(tile_rows * f + tile_rows - 1, 1)
                if f >= first_elem:
                    sum_along_rows(tile_rows * f, tile_rows)
                if f > first_elem:
                    sum_across_rows(f - 1)
            if e + 2 == tiles:
                sum_across_rows(tiles - 1)

        def sum_on_tensor(n):
            i, e = divmod(n, tiles)
            g = group_of[n]
            if g not in grouped:
                grouped[g] = stage.tile([P, group_sizes[g], P, PACK], BF16, align_bytes=64, name="grouped")
            sums = psum_sums.tile([P, PACK, P], F32)
            for half in range(2):
                d = 2 * e + half
                wanted = W * (2 * d - first_row(d))
                for t in range(PACK):
                    nc.tensor.matmul(
                        out=sums[:, t, half_nodes * half : half_nodes * (half + 1)],
                        lhsT=x_windows[i][:, d, t::PACK],
                        rhs=neighbours[:, wanted : wanted + half_nodes],
                        start=True,
                        stop=True,
                    )
            nc.scalar.copy(out=grouped[g][:, place_of[n], :, :], in_=sums[:].rearrange("p t n -> p n t"))

        codes = {}
        scales = {}

        def quantise(g):
            codes[g] = stage.tile([P, group_sizes[g] * P], U32, align_bytes=64, name="codes")
            scales[g] = stage.tile([P, group_sizes[g] * P], U8, align_bytes=64, name="scales")
            nc.vector.quantize_mx(
                out=codes[g][:].bitcast(FP8X4),
                scales=scales[g][:],
                in_=grouped[g][:].rearrange("p j n t -> p (j n t)"),
            )

        def multiply(n):
            g, j = group_of[n], place_of[n]
            node_cols = slice(P * j, P * (j + 1))
            banks = []
            for h in range(outputs // N_BANK):
                acc = psum_acc.tile([P, N_BANK], F32, name="acc")
                nc.tensor.matmul_mx(
                    out=acc[:],
                    lhsT=codes[g][:, node_cols].bitcast(FP8X4),
                    lhsT_scale=scales[g][:, node_cols],
                    rhs=w_words[:, 2 * N_BANK * h : 2 * N_BANK * (h + 1)].bitcast(FP4X4),
                    rhs_scale=w_scales[:, N_BANK * h : N_BANK * (h + 1)],
                    start=True,
                    stop=True,
                )
                banks.append(acc)
            return banks

        def add_bias_and_store(n, banks):
            rows = result.tile([P, outputs], F32)
            for h, acc in enumerate(banks):
                out_cols = slice(N_BANK * h, N_BANK * (h + 1))
                nc.vector.tensor_tensor(out=rows[:, out_cols], in0=acc[:], in1=bias[:, out_cols], op=ADD)
            i, e = divmod(n, tiles)
            nc.sync.dma_start(out=out[i, P * e : P * (e + 1), :], in_=rows[:])

        def summed_by(n):
            return min(2 * n + 4, n + LEAD + 1, tensor_tiles)

        transpose_last(0)
        sum_elementwise(0)
        turn_bias()
        spread_bias()
        for k in range(summed_by(-1)):
            sum_on_tensor(k)
        transpose_last(2)
        sum_elementwise(2)
        quantise(0)
        for n in range(all_tiles):
            banks = multiply(n)
            for k in range(summed_by(n - 1), summed_by(n)):
                sum_on_tensor(k)
            if n % 2 == 0 and 4 <= n + 2 < tiles:
                transpose_last(n + 2)
                sum_elementwise(n + 2)
            if n + 1 in first_tile:
                quantise(group_of[n + 1])
            add_bias_and_store(n, banks)
